import numpy as np
import ml_dtypes


def mxq(x, axis, fmt="e4m3"):
    dtype, down = {"e4m3": (ml_dtypes.float8_e4m3fn, 7), "e5m2": (ml_dtypes.float8_e5m2, 14)}[fmt]
    v = np.moveaxis(np.asarray(x, np.float32).astype(ml_dtypes.bfloat16).astype(np.float64), axis, -1)
    blocks = v.reshape(v.shape[:-1] + (-1, 32))
    amax = np.abs(blocks).max(-1, keepdims=True)
    byte = np.maximum(np.where(amax > 0, np.frexp(amax)[1] - 1 + 127, 0) - down, 1)
    scale = np.exp2(byte - 127.0)
    codes = (blocks / scale).astype(np.float32).astype(dtype).astype(np.float64)
    return np.moveaxis((codes * scale).reshape(v.shape), -1, axis)


WIDE = False


def mx_kscale(k):
    if not WIDE:
        return np.ones(k)
    levels = np.array([10, -10, 5, -5, 0])
    a = np.random.permutation(np.resize(levels, k // 512 * 4)).reshape(k // 512, 4)
    idx = np.arange(k)
    return np.exp2(a[idx // 512, idx % 128 // 32])


BF16 = ml_dtypes.bfloat16


def bf(x):
    return np.asarray(x, np.float32).astype(BF16)


def f64(x):
    return np.asarray(x).astype(np.float64)


E2M1 = np.array([0.0, 0.5, 1.0, 1.5, 2.0, 3.0, 4.0, 6.0, -0.0, -0.5, -1.0, -1.5, -2.0, -3.0, -4.0, -6.0])


def pack_weight(w, fmt):
    k, n = w.shape
    w = f64(bf(w)).reshape(k // 32, 32, n)
    amax = np.abs(w).max(1)
    if fmt == "e4m3":
        byte = np.frexp(amax)[1] - 1 + 127 - 7
    else:
        mant, ex = np.frexp(amax / 6.0)
        byte = np.where(mant > 0.5, ex, ex - 1) + 127
    byte = np.clip(np.where(amax > 0, byte, 1), 1, 254)
    scaled = (w * np.exp2(127.0 - byte)[:, None, :]).reshape(k, n).astype(np.float32)
    by_word = np.ascontiguousarray(scaled.reshape(k // 512, 128, 4, n).transpose(0, 1, 3, 2))
    if fmt == "e4m3":
        words = by_word.astype(ml_dtypes.float8_e4m3fn).view(np.uint8)
    else:
        c = by_word.astype(ml_dtypes.float4_e2m1fn).view(np.uint8) & 0xF
        words = c[..., 0::2] | (c[..., 1::2] << 4)
    return np.ascontiguousarray(words), np.ascontiguousarray(byte.astype(np.uint8).reshape(k // 512, 16, n))


def unpack_weight(words, scales, fmt):
    g, p, n, _ = words.shape
    if fmt == "e4m3":
        vals = np.ascontiguousarray(words).view(ml_dtypes.float8_e4m3fn).astype(np.float64)
    else:
        nib = np.empty((g, p, n, 4), np.uint8)
        nib[..., 0::2] = words & 0xF
        nib[..., 1::2] = words >> 4
        vals = E2M1[nib]
    vals = vals * np.repeat(np.exp2(scales.astype(np.float64) - 127.0), 8, axis=1)[..., None]
    return vals.transpose(0, 1, 3, 2).reshape(g * 512, n)


B, N, D, H, DH = 4, 640, 1024, 16, 64
R = 2 * DH
EPS = 1e-12
BASE = 10000.0
FMT = "e4m3"


def l2norm(t):
    n = np.sqrt(np.sum(t * t, axis=-1, keepdims=True))
    return t / np.maximum(n, EPS)


def rotate_half(t):
    t1, t2 = np.split(t, 2, axis=-1)
    return np.concatenate([-t2, t1], axis=-1)


def rope_tables():
    inv_freq = 1.0 / (BASE ** (np.arange(0, R, 2) / R))
    freqs = np.outer(np.arange(N), inv_freq)
    emb = np.concatenate([freqs, freqs], axis=-1)
    return np.cos(emb), np.sin(emb)


def setup_inputs():
    s, t = mx_kscale(D), mx_kscale(D)
    g = np.sqrt(DH)
    x = bf(np.random.standard_normal((B, N, D)) * s)
    a = bf(np.random.standard_normal((B, N, D)) * t)
    wx_words, wx_scales = pack_weight((np.random.standard_normal((R, D)) / np.sqrt(D) / s).T, FMT)
    wa_words, wa_scales = pack_weight((np.random.standard_normal((R, D)) / np.sqrt(D) / t).T, FMT)
    kx_scale = bf(g * (1.0 + 0.1 * np.random.standard_normal((1, 1, DH))))
    ka_scale = bf(g * (1.0 + 0.1 * np.random.standard_normal((1, 1, DH))))
    return {
        "x": x,
        "a": a,
        "Wkv_x_words": wx_words,
        "Wkv_x_scales": wx_scales,
        "Wkv_a_words": wa_words,
        "Wkv_a_scales": wa_scales,
        "kx_scale": kx_scale,
        "ka_scale": ka_scale,
    }


def reference(x, a, Wkv_x_words, Wkv_x_scales, Wkv_a_words, Wkv_a_scales, kx_scale, ka_scale):
    kv_x = mxq(f64(x), 2, "e4m3") @ unpack_weight(Wkv_x_words, Wkv_x_scales, FMT)
    kv_a = mxq(f64(a), 2, "e4m3") @ unpack_weight(Wkv_a_words, Wkv_a_scales, FMT)
    k_x, v_x = np.split(kv_x[:, None], 2, axis=-1)
    k_a, v_a = np.split(kv_a[:, None], 2, axis=-1)
    k_x = l2norm(k_x) * f64(kx_scale)
    k_a = l2norm(k_a) * f64(ka_scale)
    k = np.concatenate([k_x, k_a], axis=-1)
    v = np.concatenate([v_x, v_a], axis=-1)
    cos, sin = rope_tables()
    k = k * cos + rotate_half(k) * sin
    return k[:, 0], v[:, 0]

@@ -1,0 +1,429 @@
+import math
+from contextlib import ExitStack
+
+import concourse.mybir as mybir
+from concourse.masks import make_identity
+
+F32 = mybir.dt.float32
+BF16 = mybir.dt.bfloat16
+I32 = mybir.dt.int32
+U32 = mybir.dt.uint32
+U8 = mybir.dt.uint8
+FP8X4 = mybir.dt.float8_e4m3fn_x4
+ACT = mybir.ActivationFunctionType
+ALU = mybir.AluOpType
+
+P = 128
+BATCH = 4
+TOKENS = 640
+D_MODEL = 1024
+HEAD = 64
+KV = 2 * HEAD
+STREAMS = 2
+K_PASS = 4 * P
+PASSES = D_MODEL // K_PASS
+HALVES = 2
+TILES_PER_BATCH = TOKENS // P
+ROUND_TILES = 2
+ROUNDS = BATCH * TILES_PER_BATCH // ROUND_TILES
+TILEWISE_BATCHES = 2
+FIRST_PIECE = 2
+ROPE_BASE = 10000.0
+GROWTH_WIDTHS = (1, 4, 16)
+EPS_SQUARED = 1e-12 * 1e-12
+ROUND_MAGIC = 1.5 * 2.0**23
+
+FLOPS = 2 * STREAMS * BATCH * TOKENS * D_MODEL * KV
+
+
+def tile_cmattention_pb_kernel(
+    tc, x, a, Wkv_x_words, Wkv_x_scales, Wkv_a_words, Wkv_a_scales, kx_scale, ka_scale, out_0, out_1
+):
+    nc = tc.nc
+    streams = (x, a)
+    weight_words = (Wkv_x_words, Wkv_a_words)
+    weight_scales = (Wkv_x_scales, Wkv_a_scales)
+    gain_rows = (kx_scale, ka_scale)
+
+    with ExitStack() as ctx:
+        consts = ctx.enter_context(tc.tile_pool(name="consts", bufs=1))
+        resident = ctx.enter_context(tc.tile_pool(name="resident", bufs=1))
+        stage = ctx.enter_context(tc.tile_pool(name="stage", bufs=2))
+        small = ctx.enter_context(tc.tile_pool(name="small", bufs=3))
+        psum_t = ctx.enter_context(tc.psum_pool(name="psum_t", bufs=5))
+        psum_kv = ctx.enter_context(tc.psum_pool(name="psum_kv", bufs=3))
+        ctx.enter_context(tc.manual_schedule())
+
+        acts = [
+            [
+                resident.tile([P, TILES_PER_BATCH, D_MODEL], BF16, name="act_%d_%d" % (s, b))
+                for b in range(BATCH)
+            ]
+            for s in range(STREAMS)
+        ]
+
+        def load_tokens(b, first, last):
+            for s in range(STREAMS):
+                nc.sync.dma_start(
+                    out=acts[s][b][:, first:last, :],
+                    in_=streams[s][b].rearrange("(p i) d -> p i d", i=TILES_PER_BATCH)[:, first:last, :],
+                )
+
+        w_planes = consts.tile([P, STREAMS, PASSES, KV], U8, align_bytes=64)
+        nc.vector.memset(w_planes[:].rearrange("p s g n -> p (s g n)").bitcast(I32), 0)
+
+        def load_scale_rows(s, quadrant):
+            nc.sync.dma_start(
+                out=w_planes[32 * quadrant : 32 * quadrant + 4, s, :, :].bitcast(I32),
+                in_=weight_scales[s][:, 4 * quadrant : 4 * quadrant + 4, :]
+                .rearrange("g r n -> r g n")
+                .bitcast(I32),
+            )
+
+        gains_on_row_0 = consts.tile([P, STREAMS, HEAD], BF16)
+        nc.gpsimd.memset(gains_on_row_0[:], 0.0)
+        all_ones = consts.tile([P, P], BF16)
+        nc.gpsimd.memset(all_ones[:], 1.0)
+        w_codes = consts.tile([P, STREAMS, PASSES, 4 * KV], U8, align_bytes=64)
+        scale_loads = [(s, quadrant) for s in range(STREAMS) for quadrant in range(4)]
+        for i in range(TILES_PER_BATCH):
+            load_tokens(0, i, i + 1)
+            if i == 0:
+                for s in range(STREAMS):
+                    nc.sync.dma_start(out=gains_on_row_0[0:1, s, :], in_=gain_rows[s][0, :, :])
+            if i == ROUND_TILES - 1:
+                for s in range(STREAMS):
+                    nc.sync.dma_start(
+                        out=w_codes[:, s, :, :].bitcast(I32),
+                        in_=weight_words[s].rearrange("g p n t -> p g (n t)").bitcast(I32),
+                    )
+            for s, quadrant in scale_loads[2 * i : 2 * i + 2]:
+                load_scale_rows(s, quadrant)
+        for b in range(1, TILEWISE_BATCHES):
+            for i in range(TILES_PER_BATCH):
+                load_tokens(b, i, i + 1)
+        for b in range(TILEWISE_BATCHES, BATCH):
+            first = 0
+            while first < TILES_PER_BATCH:
+                end = min(first + ROUND_TILES - (TILES_PER_BATCH * b + first) % ROUND_TILES, TILES_PER_BATCH)
+                load_tokens(b, first, end)
+                first = end
+
+        identity = consts.tile([P, P], F32)
+        make_identity(nc, identity[:])
+        position_int = consts.tile([P, TILES_PER_BATCH], I32)
+        nc.gpsimd.iota(position_int[:], pattern=[[1, TILES_PER_BATCH]], base=0, channel_multiplier=TILES_PER_BATCH)
+
+        floor_plus = consts.tile([P, 1], F32)
+        floor_minus = consts.tile([P, 1], F32)
+        nc.vector.memset(floor_plus[:], EPS_SQUARED)
+        nc.vector.memset(floor_minus[:], -EPS_SQUARED)
+
+        warm = consts.tile([P, 2], F32)
+        nc.scalar.activation(out=warm[:, 0:1], in_=floor_plus[:], func=ACT.Sin)
+
+        inv_freq = consts.tile([P, HEAD], F32)
+        nc.vector.memset(inv_freq[:, 0:1], 1.0)
+        for width in GROWTH_WIDTHS:
+            for m in range(1, 4):
+                nc.vector.tensor_scalar(
+                    out=inv_freq[:, m * width : (m + 1) * width],
+                    in0=inv_freq[:, 0:width],
+                    scalar1=ROPE_BASE ** (-m * width / HEAD),
+                    scalar2=None,
+                    op0=ALU.mult,
+                )
+        position = consts.tile([P, TILES_PER_BATCH], F32)
+        nc.vector.tensor_copy(out=position[:], in_=position_int[:])
+        table_shape = [P, TILES_PER_BATCH, HEAD]
+        theta = consts.tile(table_shape, F32)
+        nc.vector.tensor_tensor(
+            out=theta[:],
+            in0=inv_freq[:].unsqueeze(1).to_broadcast(table_shape),
+            in1=position[:].unsqueeze(2).to_broadcast(table_shape),
+            op=ALU.mult,
+        )
+        turns = consts.tile([P, TILES_PER_BATCH, 2, HEAD], F32)
+        for plane, ahead in ((0, 0.25), (1, 0.0)):
+            nc.vector.tensor_scalar(
+                out=turns[:, :, plane, :],
+                in0=theta[:],
+                scalar1=1.0 / (2.0 * math.pi),
+                scalar2=ahead,
+                op0=ALU.mult,
+                op1=ALU.add,
+            )
+        whole = consts.tile([P, TILES_PER_BATCH, 2, HEAD], F32)
+        nc.vector.tensor_scalar(
+            out=whole[:], in0=turns[:], scalar1=ROUND_MAGIC, scalar2=ROUND_MAGIC, op0=ALU.add, op1=ALU.subtract
+        )
+        fraction = consts.tile([P, TILES_PER_BATCH, 2, HEAD], F32)
+        nc.vector.tensor_tensor(out=fraction[:], in0=turns[:], in1=whole[:], op=ALU.subtract)
+        cos_sin = consts.tile([P, TILES_PER_BATCH, 2, HEAD], F32)
+
+        def take_sines():
+            nc.scalar.activation(out=cos_sin[:], in_=fraction[:], func=ACT.Sin, scale=2.0 * math.pi)
+            nc.scalar.activation(out=warm[:, 1:2], in_=inv_freq[:, 0:1], func=ACT.Abs_reciprocal_sqrt)
+
+        rope = consts.tile([P, TILES_PER_BATCH, STREAMS, 2, HEAD], F32)
+
+        spread = {}
+
+        def spread_gains():
+            bank = psum_kv.tile([P, ROUND_TILES, STREAMS, KV], F32, name="product")
+            nc.tensor.matmul(
+                out=bank[:, 0, 0, :],
+                lhsT=all_ones[:],
+                rhs=gains_on_row_0[:].rearrange("p s j -> p (s j)"),
+                start=True,
+                stop=True,
+            )
+            spread["gains"] = bank[:, 0, 0, :].rearrange("p (s j) -> p s j", s=STREAMS)
+
+        def finish_tables():
+            gains = spread["gains"]
+            nc.vector.tensor_tensor(
+                out=rope[:, :, 0, :, :],
+                in0=cos_sin[:],
+                in1=gains[:, 0, :].unsqueeze(1).unsqueeze(1).to_broadcast([P, TILES_PER_BATCH, 2, HEAD]),
+                op=ALU.mult,
+            )
+            gain_a = gains[:, 1, :].unsqueeze(1).to_broadcast(table_shape)
+            nc.vector.scalar_tensor_tensor(
+                out=rope[:, :, 1, 0, :], in0=cos_sin[:, :, 1, :], scalar=-1.0, in1=gain_a, op0=ALU.mult, op1=ALU.mult
+            )
+            nc.vector.tensor_tensor(out=rope[:, :, 1, 1, :], in0=cos_sin[:, :, 0, :], in1=gain_a, op=ALU.mult)
+
+        last = ROUNDS - 1
+        k_all = resident.tile([P, BATCH * TILES_PER_BATCH, KV], F32)
+        v_all = resident.tile([P, BATCH * TILES_PER_BATCH, KV], F32)
+        transposed = {}
+        grouped = {}
+        codes = {}
+        planes = {}
+        products = {}
+        product_bank = {}
+        inv_norm = {}
+        squares = {}
+        unread = {}
+        shares = {}
+
+        sorted_words = {}
+
+        def sort_words(r, t, s):
+            b, i = divmod(ROUND_TILES * r + t, TILES_PER_BATCH)
+            flat = stage.tile([P, PASSES, HALVES, P], F32, name="flat")
+            nc.vector.tensor_copy(
+                out=flat[:],
+                in_=acts[s][b][:, i, :].bitcast(F32).rearrange("p (g m u) -> p g u m", g=PASSES, u=HALVES),
+            )
+            sorted_words[(r, t, s)] = flat
+
+        def transpose_round(r):
+            for t in range(ROUND_TILES):
+                b, i = divmod(ROUND_TILES * r + t, TILES_PER_BATCH)
+                for s in range(STREAMS):
+                    words = acts[s][b][:, i, :].bitcast(F32)
+                    bank = psum_t.tile([P, PASSES, HALVES, P], F32, name="bank")
+                    for g in range(PASSES):
+                        for u in range(HALVES):
+                            first = g * K_PASS // 2 + u
+                            if (r, t, s) in sorted_words:
+                                source = sorted_words[(r, t, s)][:, g, u, :]
+                            else:
+                                source = words[:, first : (g + 1) * K_PASS // 2 : HALVES]
+                            nc.tensor.transpose(out=bank[:, g, u, :], in_=source, identity=identity[:])
+                    transposed[(r, t, s)] = bank
+            grouped[r] = stage.tile([P, ROUND_TILES, STREAMS, D_MODEL], BF16, name="grouped", align_bytes=64)
+
+        def empty_bank(copy, r, t, s):
+            copy(
+                out=grouped[r][:, t, s, :].bitcast(F32).rearrange("p (g n u) -> p g n u", g=PASSES, u=HALVES),
+                in_=transposed[(r, t, s)][:].rearrange("p g u n -> p g n u"),
+            )
+
+        def quantise(r, t, first, count):
+            if r not in codes:
+                codes[r] = stage.tile([P, ROUND_TILES, STREAMS, D_MODEL // 4], U32, name="codes", align_bytes=64)
+                planes[r] = stage.tile([P, ROUND_TILES, STREAMS, D_MODEL // 4], U8, name="planes", align_bytes=64)
+            some = slice(first, first + count)
+            nc.vector.quantize_mx(
+                out=codes[r][:, t, some, :].rearrange("p s w -> p (s w)").bitcast(FP8X4),
+                scales=planes[r][:, t, some, :].rearrange("p s w -> p (s w)"),
+                in_=grouped[r][:, t, some, :].rearrange("p s k -> p (s k)"),
+            )
+
+        def multiply(r):
+            bank = psum_kv.tile([P, ROUND_TILES, STREAMS, KV], F32, name="product")
+            product_bank[r] = bank
+            products[(r, 0)] = bank[:, 0, :, :]
+            products[(r, 1)] = bank[:, 1, :, :]
+            if r == last:
+                other = psum_t.tile([P, PASSES, HALVES, P], F32, name="bank")
+                products[(r, 1)] = other[:, 1, :, :]
+            for t in range(ROUND_TILES):
+                for s in range(STREAMS):
+                    for g in range(PASSES):
+                        tokens = slice(g * P, (g + 1) * P)
+                        nc.tensor.matmul_mx(
+                            out=products[(r, t)][:, s, :],
+                            lhsT=codes[r][:, t, s, tokens].bitcast(FP8X4),
+                            lhsT_scale=planes[r][:, t, s, tokens],
+                            rhs=w_codes[:, s, g, :].bitcast(FP8X4),
+                            rhs_scale=w_planes[:, s, g, :],
+                            start=(g == 0),
+                            stop=(g == PASSES - 1),
+                        )
+
+        def sum_squares(r, t):
+            if r not in squares:
+                squares[r] = small.tile([P, 2, ROUND_TILES * STREAMS], F32, name="square_sums")
+                unread[r] = stage.tile([P, ROUND_TILES, STREAMS, HEAD], F32, name="unread")
+                inv_norm[r] = small.tile([P, ROUND_TILES * STREAMS], F32, name="inverse_norms")
+            for s in range(STREAMS):
+                column = STREAMS * t + s
+                nc.scalar.activation(
+                    out=unread[r][:, t, s, :],
+                    in_=products[(r, t)][:, s, 0:HEAD],
+                    func=ACT.Square,
+                    accum_out=squares[r][:, 0, column : column + 1],
+                )
+
+        def apply_floor(r, first, count):
+            columns = slice(STREAMS * first, STREAMS * (first + count))
+            nc.scalar.activation(
+                out=squares[r][:, 1, columns], in_=squares[r][:, 0, columns], func=ACT.Relu, bias=floor_minus[:]
+            )
+
+        def invert_norms(r, first, count):
+            columns = slice(STREAMS * first, STREAMS * (first + count))
+            nc.scalar.activation(
+                out=inv_norm[r][:, columns], in_=squares[r][:, 1, columns], func=ACT.Abs_reciprocal_sqrt, bias=floor_plus[:]
+            )
+
+        def rotate(r, t):
+            if r not in shares:
+                shares[r] = stage.tile([P, ROUND_TILES, STREAMS, 2, HEAD], F32, name="share")
+            i = (ROUND_TILES * r + t) % TILES_PER_BATCH
+            for s in range(STREAMS):
+                column = STREAMS * t + s
+                nc.vector.scalar_tensor_tensor(
+                    out=shares[r][:, t, s, :, :],
+                    in0=products[(r, t)][:, s, 0:HEAD].unsqueeze(1).to_broadcast([P, 2, HEAD]),
+                    scalar=inv_norm[r][:, column : column + 1],
+                    in1=rope[:, i, s, :, :],
+                    op0=ALU.mult,
+                    op1=ALU.mult,
+                )
+
+        def add_shares(engine, r, first, count):
+            some = slice(first, first + count)
+            engine.tensor_tensor(
+                out=k_all[:, ROUND_TILES * r + first : ROUND_TILES * r + first + count, :],
+                in0=shares[r][:, some, 0, :, :].rearrange("p t h j -> p t (h j)"),
+                in1=shares[r][:, some, 1, :, :].rearrange("p t h j -> p t (h j)"),
+                op=ALU.add,
+            )
+
+        def copy_values(r):
+            nc.scalar.copy(
+                out=v_all[:, ROUND_TILES * r : ROUND_TILES * (r + 1), :].rearrange("p t (s j) -> p t s j", s=STREAMS),
+                in_=product_bank[r][:, :, :, HEAD:KV],
+            )
+
+        def copy_values_of_tile(r, t):
+            nc.scalar.copy(
+                out=v_all[:, ROUND_TILES * r + t, :].rearrange("p (s j) -> p s j", s=STREAMS),
+                in_=products[(r, t)][:, :, HEAD:KV],
+            )
+
+        pieces = [(TILES_PER_BATCH * b, TILES_PER_BATCH * (b + 1)) for b in range(BATCH - 1)]
+        pieces.append((TILES_PER_BATCH * (BATCH - 1), ROUND_TILES * last))
+        pieces.append((ROUND_TILES * last, BATCH * TILES_PER_BATCH))
+
+        held_back = []
+        first_to_go = ROUNDS - 3
+
+        def store(out, result, first, end):
+            b, i = divmod(first, TILES_PER_BATCH)
+            nc.sync.dma_start(
+                out=out[b].rearrange("(p i) c -> p i c", i=TILES_PER_BATCH)[:, i : i + end - first, :],
+                in_=result[:, first:end, :],
+            )
+
+        def store_finished(out, result, r):
+            for first, end in pieces:
+                if (end - 1) // ROUND_TILES == r:
+                    if r < first_to_go:
+                        held_back.append((out, result, first, end))
+                    else:
+                        store(out, result, first, end)
+                        for earlier in held_back:
+                            store(earlier[0], earlier[1], earlier[2], earlier[3])
+                        held_back.clear()
+
+        for step in range(ROUNDS + 1):
+            transposing = step < ROUNDS
+            multiplying = 0 <= step - 1
+            norming = 0 <= step - 2
+            closing = 0 <= step - 3
+            if transposing:
+                transpose_round(step)
+            if step == 0:
+                spread_gains()
+            if multiplying:
+                if step - 1 == last:
+                    quantise(last, 1, 0, 1)
+                    quantise(last, 1, 1, 1)
+                else:
+                    quantise(step - 1, 1, 0, STREAMS)
+                multiply(step - 1)
+
+            if norming:
+                sum_squares(step - 2, 0)
+                sum_squares(step - 2, 1)
+                if transposing:
+                    copy_values_of_tile(step - 2, 0)
+                apply_floor(step - 2, 0, ROUND_TILES)
+                if transposing:
+                    copy_values_of_tile(step - 2, 1)
+                    store_finished(out_1, v_all, step - 2)
+                invert_norms(step - 2, 0, ROUND_TILES)
+            if step == ROUNDS:
+                for t in range(ROUND_TILES):
+                    sum_squares(last, t)
+                    apply_floor(last, t, 1)
+                    invert_norms(last, t, 1)
+            if transposing:
+                empty_bank(nc.scalar.copy, step, 0, 1)
+                empty_bank(nc.scalar.copy, step, 1, 0)
+                empty_bank(nc.scalar.copy, step, 1, 1)
+            if step == 0:
+                take_sines()
+
+            if closing:
+                rotate(step - 3, 1)
+                add_shares(nc.gpsimd, step - 3, 0, ROUND_TILES)
+                store_finished(out_0, k_all, step - 3)
+            if transposing:
+                empty_bank(nc.vector.tensor_copy, step, 0, 0)
+            if step == 1:
+                finish_tables()
+            if norming:
+                rotate(step - 2, 0)
+            if transposing:
+                quantise(step, 0, 0, STREAMS)
+            if 2 <= step + 1 < ROUNDS - 3:
+                sort_words(step + 1, 1, 1)
+            if step == ROUNDS:
+                rotate(step - 2, 1)
+                add_shares(nc.gpsimd, step - 2, 0, ROUND_TILES)
+                store_finished(out_0, k_all, step - 2)
+                copy_values(step - 2)
+                store_finished(out_1, v_all, step - 2)
+                for t in range(ROUND_TILES):
+                    rotate(last, t)
+                    copy_values_of_tile(last, t)
+                add_shares(nc.vector, last, 0, ROUND_TILES)
+                store_finished(out_0, k_all, last)
+                store_finished(out_1, v_all, last)

@@ -26,7 +26,7 @@ HALVES = 2
 TILES_PER_BATCH = TOKENS // P
 ROUND_TILES = 2
 ROUNDS = BATCH * TILES_PER_BATCH // ROUND_TILES
-TILEWISE_BATCHES = 2
+ROUNDWISE_BATCHES = 2
 FIRST_PIECE = 2
 ROPE_BASE = 10000.0
 GROWTH_WIDTHS = (1, 4, 16)
@@ -90,7 +90,7 @@ def tile_cmattention_pb_kernel(
             load_tokens(0, i, i + 1)
             if i == 0:
                 for s in range(STREAMS):
-                    nc.sync.dma_start(out=gains_on_row_0[0:1, s, :], in_=gain_rows[s][0, :, :])
+                    nc.gpsimd.dma_start(out=gains_on_row_0[0:1, s, :], in_=gain_rows[s][0, :, :])
             if i == ROUND_TILES - 1:
                 for s in range(STREAMS):
                     nc.sync.dma_start(
@@ -99,15 +99,15 @@ def tile_cmattention_pb_kernel(
                     )
             for s, quadrant in scale_loads[2 * i : 2 * i + 2]:
                 load_scale_rows(s, quadrant)
-        for b in range(1, TILEWISE_BATCHES):
-            for i in range(TILES_PER_BATCH):
-                load_tokens(b, i, i + 1)
-        for b in range(TILEWISE_BATCHES, BATCH):
+        for b in range(1, ROUNDWISE_BATCHES):
             first = 0
             while first < TILES_PER_BATCH:
                 end = min(first + ROUND_TILES - (TILES_PER_BATCH * b + first) % ROUND_TILES, TILES_PER_BATCH)
                 load_tokens(b, first, end)
                 first = end
+        for b in range(ROUNDWISE_BATCHES, BATCH):
+            load_tokens(b, 0, FIRST_PIECE)
+            load_tokens(b, FIRST_PIECE, TILES_PER_BATCH)
 
         identity = consts.tile([P, P], F32)
         make_identity(nc, identity[:])

@@ -90,7 +90,7 @@ def tile_cmattention_pb_kernel(
             load_tokens(0, i, i + 1)
             if i == 0:
                 for s in range(STREAMS):
-                    nc.gpsimd.dma_start(out=gains_on_row_0[0:1, s, :], in_=gain_rows[s][0, :, :])
+                    nc.sync.dma_start(out=gains_on_row_0[0:1, s, :], in_=gain_rows[s][0, :, :])
             if i == ROUND_TILES - 1:
                 for s in range(STREAMS):
                     nc.sync.dma_start(

@@ -325,24 +325,20 @@ def tile_cmattention_pb_kernel(
                 op=ALU.add,
             )
 
-        def copy_values(r):
-            nc.scalar.copy(
-                out=v_all[:, ROUND_TILES * r : ROUND_TILES * (r + 1), :].rearrange("p t (s j) -> p t s j", s=STREAMS),
-                in_=product_bank[r][:, :, :, HEAD:KV],
-            )
-
         def copy_values_of_tile(r, t):
             nc.scalar.copy(
                 out=v_all[:, ROUND_TILES * r + t, :].rearrange("p (s j) -> p s j", s=STREAMS),
                 in_=products[(r, t)][:, :, HEAD:KV],
             )
 
-        pieces = [(TILES_PER_BATCH * b, TILES_PER_BATCH * (b + 1)) for b in range(BATCH - 1)]
+        pieces = [(TILES_PER_BATCH * b, TILES_PER_BATCH * (b + 1)) for b in range(BATCH - 2)]
+        first_to_go = ROUNDS - 4
+        pieces.append((TILES_PER_BATCH * (BATCH - 2), ROUND_TILES * (first_to_go + 1)))
+        pieces.append((ROUND_TILES * (first_to_go + 1), TILES_PER_BATCH * (BATCH - 1)))
         pieces.append((TILES_PER_BATCH * (BATCH - 1), ROUND_TILES * last))
         pieces.append((ROUND_TILES * last, BATCH * TILES_PER_BATCH))
 
         held_back = []
-        first_to_go = ROUNDS - 3
 
         def store(out, result, first, end):
             b, i = divmod(first, TILES_PER_BATCH)
@@ -382,18 +378,19 @@ def tile_cmattention_pb_kernel(
             if norming:
                 sum_squares(step - 2, 0)
                 sum_squares(step - 2, 1)
-                if transposing:
-                    copy_values_of_tile(step - 2, 0)
+                copy_values_of_tile(step - 2, 0)
                 apply_floor(step - 2, 0, ROUND_TILES)
-                if transposing:
-                    copy_values_of_tile(step - 2, 1)
-                    store_finished(out_1, v_all, step - 2)
+                copy_values_of_tile(step - 2, 1)
+                store_finished(out_1, v_all, step - 2)
                 invert_norms(step - 2, 0, ROUND_TILES)
             if step == ROUNDS:
-                for t in range(ROUND_TILES):
-                    sum_squares(last, t)
-                    apply_floor(last, t, 1)
-                    invert_norms(last, t, 1)
+                sum_squares(last, 0)
+                sum_squares(last, 1)
+                copy_values_of_tile(last, 0)
+                apply_floor(last, 0, ROUND_TILES)
+                copy_values_of_tile(last, 1)
+                store_finished(out_1, v_all, last)
+                invert_norms(last, 0, ROUND_TILES)
             if transposing:
                 empty_bank(nc.scalar.copy, step, 0, 1)
                 empty_bank(nc.scalar.copy, step, 1, 0)
@@ -419,11 +416,8 @@ def tile_cmattention_pb_kernel(
                 rotate(step - 2, 1)
                 add_shares(nc.gpsimd, step - 2, 0, ROUND_TILES)
                 store_finished(out_0, k_all, step - 2)
-                copy_values(step - 2)
-                store_finished(out_1, v_all, step - 2)
                 for t in range(ROUND_TILES):
                     rotate(last, t)
-                    copy_values_of_tile(last, t)
-                add_shares(nc.vector, last, 0, ROUND_TILES)
+                for t in range(ROUND_TILES):
+                    add_shares(nc.vector, last, t, 1)
                 store_finished(out_0, k_all, last)
-                store_finished(out_1, v_all, last)

@@ -26,8 +26,8 @@ HALVES = 2
 TILES_PER_BATCH = TOKENS // P
 ROUND_TILES = 2
 ROUNDS = BATCH * TILES_PER_BATCH // ROUND_TILES
-ROUNDWISE_BATCHES = 2
-FIRST_PIECE = 2
+UNITS = ROUND_TILES * STREAMS
+LOADS = (((0, 1), (1, 2), (2, 4), (4, 5)), ((0, 1), (1, 3), (3, 5)), ((0, 2), (2, 5)), ((0, 2), (2, 5)))
 ROPE_BASE = 10000.0
 GROWTH_WIDTHS = (1, 4, 16)
 EPS_SQUARED = 1e-12 * 1e-12
@@ -62,12 +62,11 @@ def tile_cmattention_pb_kernel(
             for s in range(STREAMS)
         ]
 
-        def load_tokens(b, first, last):
-            for s in range(STREAMS):
-                nc.sync.dma_start(
-                    out=acts[s][b][:, first:last, :],
-                    in_=streams[s][b].rearrange("(p i) d -> p i d", i=TILES_PER_BATCH)[:, first:last, :],
-                )
+        def load_tokens(s, b, first, end):
+            nc.sync.dma_start(
+                out=acts[s][b][:, first:end, :],
+                in_=streams[s][b].rearrange("(p i) d -> p i d", i=TILES_PER_BATCH)[:, first:end, :],
+            )
 
         w_planes = consts.tile([P, STREAMS, PASSES, KV], U8, align_bytes=64)
         nc.vector.memset(w_planes[:].rearrange("p s g n -> p (s g n)").bitcast(I32), 0)
@@ -86,28 +85,22 @@ def tile_cmattention_pb_kernel(
         nc.gpsimd.memset(all_ones[:], 1.0)
         w_codes = consts.tile([P, STREAMS, PASSES, 4 * KV], U8, align_bytes=64)
         scale_loads = [(s, quadrant) for s in range(STREAMS) for quadrant in range(4)]
-        for i in range(TILES_PER_BATCH):
-            load_tokens(0, i, i + 1)
-            if i == 0:
+        scales_behind = {(0, 0): scale_loads[0:2], (0, 1): scale_loads[2:4], (0, 2): scale_loads[4:8]}
+        for b in range(BATCH):
+            for first, end in LOADS[b]:
                 for s in range(STREAMS):
-                    nc.sync.dma_start(out=gains_on_row_0[0:1, s, :], in_=gain_rows[s][0, :, :])
-            if i == ROUND_TILES - 1:
-                for s in range(STREAMS):
-                    nc.sync.dma_start(
-                        out=w_codes[:, s, :, :].bitcast(I32),
-                        in_=weight_words[s].rearrange("g p n t -> p g (n t)").bitcast(I32),
-                    )
-            for s, quadrant in scale_loads[2 * i : 2 * i + 2]:
-                load_scale_rows(s, quadrant)
-        for b in range(1, ROUNDWISE_BATCHES):
-            first = 0
-            while first < TILES_PER_BATCH:
-                end = min(first + ROUND_TILES - (TILES_PER_BATCH * b + first) % ROUND_TILES, TILES_PER_BATCH)
-                load_tokens(b, first, end)
-                first = end
-        for b in range(ROUNDWISE_BATCHES, BATCH):
-            load_tokens(b, 0, FIRST_PIECE)
-            load_tokens(b, FIRST_PIECE, TILES_PER_BATCH)
+                    load_tokens(s, b, first, end)
+                    if (b, first, s) == (0, 0, 0):
+                        for gain in range(STREAMS):
+                            nc.sync.dma_start(out=gains_on_row_0[0:1, gain, :], in_=gain_rows[gain][0, :, :])
+                if (b, first) == (0, 1):
+                    for s in range(STREAMS):
+                        nc.sync.dma_start(
+                            out=w_codes[:, s, :, :].bitcast(I32),
+                            in_=weight_words[s].rearrange("g p n t -> p g (n t)").bitcast(I32),
+                        )
+                for s, quadrant in scales_behind.get((b, first), []):
+                    load_scale_rows(s, quadrant)
 
         identity = consts.tile([P, P], F32)
         make_identity(nc, identity[:])
@@ -202,7 +195,6 @@ def tile_cmattention_pb_kernel(
         codes = {}
         planes = {}
         products = {}
-        product_bank = {}
         inv_norm = {}
         squares = {}
         unread = {}
@@ -210,7 +202,15 @@ def tile_cmattention_pb_kernel(
 
         sorted_words = {}
 
-        def sort_words(r, t, s):
+        def units(r):
+            b, i = divmod(ROUND_TILES * r, TILES_PER_BATCH)
+            together = any(first <= i and i + ROUND_TILES <= end for first, end in LOADS[b])
+            if together and r != last:
+                return [(t, s) for s in range(STREAMS) for t in range(ROUND_TILES)]
+            return [(t, s) for t in range(ROUND_TILES) for s in range(STREAMS)]
+
+        def sort_words(r, unit):
+            t, s = units(r)[unit]
             b, i = divmod(ROUND_TILES * r + t, TILES_PER_BATCH)
             flat = stage.tile([P, PASSES, HALVES, P], F32, name="flat")
             nc.vector.tensor_copy(
@@ -220,60 +220,57 @@ def tile_cmattention_pb_kernel(
             sorted_words[(r, t, s)] = flat
 
         def transpose_round(r):
-            for t in range(ROUND_TILES):
+            for unit, (t, s) in enumerate(units(r)):
                 b, i = divmod(ROUND_TILES * r + t, TILES_PER_BATCH)
-                for s in range(STREAMS):
-                    words = acts[s][b][:, i, :].bitcast(F32)
-                    bank = psum_t.tile([P, PASSES, HALVES, P], F32, name="bank")
-                    for g in range(PASSES):
-                        for u in range(HALVES):
-                            first = g * K_PASS // 2 + u
-                            if (r, t, s) in sorted_words:
-                                source = sorted_words[(r, t, s)][:, g, u, :]
-                            else:
-                                source = words[:, first : (g + 1) * K_PASS // 2 : HALVES]
-                            nc.tensor.transpose(out=bank[:, g, u, :], in_=source, identity=identity[:])
-                    transposed[(r, t, s)] = bank
-            grouped[r] = stage.tile([P, ROUND_TILES, STREAMS, D_MODEL], BF16, name="grouped", align_bytes=64)
+                words = acts[s][b][:, i, :].bitcast(F32)
+                bank = psum_t.tile([P, PASSES, HALVES, P], F32, name="bank")
+                for g in range(PASSES):
+                    for u in range(HALVES):
+                        first = g * K_PASS // 2 + u
+                        if (r, t, s) in sorted_words:
+                            source = sorted_words[(r, t, s)][:, g, u, :]
+                        else:
+                            source = words[:, first : (g + 1) * K_PASS // 2 : HALVES]
+                        nc.tensor.transpose(out=bank[:, g, u, :], in_=source, identity=identity[:])
+                transposed[(r, unit)] = bank
+            grouped[r] = stage.tile([P, UNITS, D_MODEL], BF16, name="grouped", align_bytes=64)
 
-        def empty_bank(copy, r, t, s):
+        def empty_bank(copy, r, unit):
             copy(
-                out=grouped[r][:, t, s, :].bitcast(F32).rearrange("p (g n u) -> p g n u", g=PASSES, u=HALVES),
-                in_=transposed[(r, t, s)][:].rearrange("p g u n -> p g n u"),
+                out=grouped[r][:, unit, :].bitcast(F32).rearrange("p (g n u) -> p g n u", g=PASSES, u=HALVES),
+                in_=transposed[(r, unit)][:].rearrange("p g u n -> p g n u"),
             )
 
-        def quantise(r, t, first, count):
+        def quantise(r, first, count):
             if r not in codes:
-                codes[r] = stage.tile([P, ROUND_TILES, STREAMS, D_MODEL // 4], U32, name="codes", align_bytes=64)
-                planes[r] = stage.tile([P, ROUND_TILES, STREAMS, D_MODEL // 4], U8, name="planes", align_bytes=64)
+                codes[r] = stage.tile([P, UNITS, D_MODEL // 4], U32, name="codes", align_bytes=64)
+                planes[r] = stage.tile([P, UNITS, D_MODEL // 4], U8, name="planes", align_bytes=64)
             some = slice(first, first + count)
             nc.vector.quantize_mx(
-                out=codes[r][:, t, some, :].rearrange("p s w -> p (s w)").bitcast(FP8X4),
-                scales=planes[r][:, t, some, :].rearrange("p s w -> p (s w)"),
-                in_=grouped[r][:, t, some, :].rearrange("p s k -> p (s k)"),
+                out=codes[r][:, some, :].rearrange("p u w -> p (u w)").bitcast(FP8X4),
+                scales=planes[r][:, some, :].rearrange("p u w -> p (u w)"),
+                in_=grouped[r][:, some, :].rearrange("p u k -> p (u k)"),
             )
 
         def multiply(r):
             bank = psum_kv.tile([P, ROUND_TILES, STREAMS, KV], F32, name="product")
-            product_bank[r] = bank
             products[(r, 0)] = bank[:, 0, :, :]
             products[(r, 1)] = bank[:, 1, :, :]
             if r == last:
                 other = psum_t.tile([P, PASSES, HALVES, P], F32, name="bank")
                 products[(r, 1)] = other[:, 1, :, :]
-            for t in range(ROUND_TILES):
-                for s in range(STREAMS):
-                    for g in range(PASSES):
-                        tokens = slice(g * P, (g + 1) * P)
-                        nc.tensor.matmul_mx(
-                            out=products[(r, t)][:, s, :],
-                            lhsT=codes[r][:, t, s, tokens].bitcast(FP8X4),
-                            lhsT_scale=planes[r][:, t, s, tokens],
-                            rhs=w_codes[:, s, g, :].bitcast(FP8X4),
-                            rhs_scale=w_planes[:, s, g, :],
-                            start=(g == 0),
-                            stop=(g == PASSES - 1),
-                        )
+            for unit, (t, s) in enumerate(units(r)):
+                for g in range(PASSES):
+                    tokens = slice(g * P, (g + 1) * P)
+                    nc.tensor.matmul_mx(
+                        out=products[(r, t)][:, s, :],
+                        lhsT=codes[r][:, unit, tokens].bitcast(FP8X4),
+                        lhsT_scale=planes[r][:, unit, tokens],
+                        rhs=w_codes[:, s, g, :].bitcast(FP8X4),
+                        rhs_scale=w_planes[:, s, g, :],
+                        start=(g == 0),
+                        stop=(g == PASSES - 1),
+                    )
 
         def sum_squares(r, t):
             if r not in squares:
@@ -369,10 +366,10 @@ def tile_cmattention_pb_kernel(
                 spread_gains()
             if multiplying:
                 if step - 1 == last:
-                    quantise(last, 1, 0, 1)
-                    quantise(last, 1, 1, 1)
+                    quantise(last, 2, 1)
+                    quantise(last, 3, 1)
                 else:
-                    quantise(step - 1, 1, 0, STREAMS)
+                    quantise(step - 1, 2, 2)
                 multiply(step - 1)
 
             if norming:
@@ -392,9 +389,8 @@ def tile_cmattention_pb_kernel(
                 store_finished(out_1, v_all, last)
                 invert_norms(last, 0, ROUND_TILES)
             if transposing:
-                empty_bank(nc.scalar.copy, step, 0, 1)
-                empty_bank(nc.scalar.copy, step, 1, 0)
-                empty_bank(nc.scalar.copy, step, 1, 1)
+                for unit in range(1, UNITS):
+                    empty_bank(nc.scalar.copy, step, unit)
             if step == 0:
                 take_sines()
 
@@ -403,15 +399,15 @@ def tile_cmattention_pb_kernel(
                 add_shares(nc.gpsimd, step - 3, 0, ROUND_TILES)
                 store_finished(out_0, k_all, step - 3)
             if transposing:
-                empty_bank(nc.vector.tensor_copy, step, 0, 0)
+                empty_bank(nc.vector.tensor_copy, step, 0)
             if step == 1:
                 finish_tables()
             if norming:
                 rotate(step - 2, 0)
             if transposing:
-                quantise(step, 0, 0, STREAMS)
+                quantise(step, 0, 2)
             if 2 <= step + 1 < ROUNDS - 3:
-                sort_words(step + 1, 1, 1)
+                sort_words(step + 1, UNITS - 1)
             if step == ROUNDS:
                 rotate(step - 2, 1)
                 add_shares(nc.gpsimd, step - 2, 0, ROUND_TILES)

import math
from contextlib import ExitStack

import concourse.mybir as mybir
from concourse.masks import make_identity

F32 = mybir.dt.float32
BF16 = mybir.dt.bfloat16
I32 = mybir.dt.int32
U32 = mybir.dt.uint32
U8 = mybir.dt.uint8
FP8X4 = mybir.dt.float8_e4m3fn_x4
ACT = mybir.ActivationFunctionType
ALU = mybir.AluOpType

P = 128
BATCH = 4
TOKENS = 640
D_MODEL = 1024
HEAD = 64
KV = 2 * HEAD
STREAMS = 2
K_PASS = 4 * P
PASSES = D_MODEL // K_PASS
HALVES = 2
TILES_PER_BATCH = TOKENS // P
ROUND_TILES = 2
ROUNDS = BATCH * TILES_PER_BATCH // ROUND_TILES
UNITS = ROUND_TILES * STREAMS
LOADS = (((0, 1), (1, 2), (2, 4), (4, 5)), ((0, 1), (1, 3), (3, 5)), ((0, 2), (2, 5)), ((0, 2), (2, 5)))
ROPE_BASE = 10000.0
GROWTH_WIDTHS = (1, 4, 16)
EPS_SQUARED = 1e-12 * 1e-12
ROUND_MAGIC = 1.5 * 2.0**23

FLOPS = 2 * STREAMS * BATCH * TOKENS * D_MODEL * KV


def tile_cmattention_pb_kernel(
    tc, x, a, Wkv_x_words, Wkv_x_scales, Wkv_a_words, Wkv_a_scales, kx_scale, ka_scale, out_0, out_1
):
    nc = tc.nc
    streams = (x, a)
    weight_words = (Wkv_x_words, Wkv_a_words)
    weight_scales = (Wkv_x_scales, Wkv_a_scales)
    gain_rows = (kx_scale, ka_scale)

    with ExitStack() as ctx:
        consts = ctx.enter_context(tc.tile_pool(name="consts", bufs=1))
        resident = ctx.enter_context(tc.tile_pool(name="resident", bufs=1))
        stage = ctx.enter_context(tc.tile_pool(name="stage", bufs=2))
        small = ctx.enter_context(tc.tile_pool(name="small", bufs=3))
        psum_t = ctx.enter_context(tc.psum_pool(name="psum_t", bufs=5))
        psum_kv = ctx.enter_context(tc.psum_pool(name="psum_kv", bufs=3))
        ctx.enter_context(tc.manual_schedule())

        acts = [
            [
                resident.tile([P, TILES_PER_BATCH, D_MODEL], BF16, name="act_%d_%d" % (s, b))
                for b in range(BATCH)
            ]
            for s in range(STREAMS)
        ]

        def load_tokens(s, b, first, end):
            nc.sync.dma_start(
                out=acts[s][b][:, first:end, :],
                in_=streams[s][b].rearrange("(p i) d -> p i d", i=TILES_PER_BATCH)[:, first:end, :],
            )

        w_planes = consts.tile([P, STREAMS, PASSES, KV], U8, align_bytes=64)
        nc.vector.memset(w_planes[:].rearrange("p s g n -> p (s g n)").bitcast(I32), 0)

        def load_scale_rows(s, quadrant):
            nc.sync.dma_start(
                out=w_planes[32 * quadrant : 32 * quadrant + 4, s, :, :].bitcast(I32),
                in_=weight_scales[s][:, 4 * quadrant : 4 * quadrant + 4, :]
                .rearrange("g r n -> r g n")
                .bitcast(I32),
            )

        gains_on_row_0 = consts.tile([P, STREAMS, HEAD], BF16)
        nc.gpsimd.memset(gains_on_row_0[:], 0.0)
        all_ones = consts.tile([P, P], BF16)
        nc.gpsimd.memset(all_ones[:], 1.0)
        w_codes = consts.tile([P, STREAMS, PASSES, 4 * KV], U8, align_bytes=64)
        scale_loads = [(s, quadrant) for s in range(STREAMS) for quadrant in range(4)]
        scales_behind = {(0, 0): scale_loads[0:2], (0, 1): scale_loads[2:4], (0, 2): scale_loads[4:8]}
        for b in range(BATCH):
            for first, end in LOADS[b]:
                for s in range(STREAMS):
                    load_tokens(s, b, first, end)
                    if (b, first, s) == (0, 0, 0):
                        for gain in range(STREAMS):
                            nc.sync.dma_start(out=gains_on_row_0[0:1, gain, :], in_=gain_rows[gain][0, :, :])
                if (b, first) == (0, 1):
                    for s in range(STREAMS):
                        nc.sync.dma_start(
                            out=w_codes[:, s, :, :].bitcast(I32),
                            in_=weight_words[s].rearrange("g p n t -> p g (n t)").bitcast(I32),
                        )
                for s, quadrant in scales_behind.get((b, first), []):
                    load_scale_rows(s, quadrant)

        identity = consts.tile([P, P], F32)
        make_identity(nc, identity[:])
        position_int = consts.tile([P, TILES_PER_BATCH], I32)
        nc.gpsimd.iota(position_int[:], pattern=[[1, TILES_PER_BATCH]], base=0, channel_multiplier=TILES_PER_BATCH)

        floor_plus = consts.tile([P, 1], F32)
        floor_minus = consts.tile([P, 1], F32)
        nc.vector.memset(floor_plus[:], EPS_SQUARED)
        nc.vector.memset(floor_minus[:], -EPS_SQUARED)

        warm = consts.tile([P, 2], F32)
        nc.scalar.activation(out=warm[:, 0:1], in_=floor_plus[:], func=ACT.Sin)

        inv_freq = consts.tile([P, HEAD], F32)
        nc.vector.memset(inv_freq[:, 0:1], 1.0)
        for width in GROWTH_WIDTHS:
            for m in range(1, 4):
                nc.vector.tensor_scalar(
                    out=inv_freq[:, m * width : (m + 1) * width],
                    in0=inv_freq[:, 0:width],
                    scalar1=ROPE_BASE ** (-m * width / HEAD),
                    scalar2=None,
                    op0=ALU.mult,
                )
        position = consts.tile([P, TILES_PER_BATCH], F32)
        nc.vector.tensor_copy(out=position[:], in_=position_int[:])
        table_shape = [P, TILES_PER_BATCH, HEAD]
        theta = consts.tile(table_shape, F32)
        nc.vector.tensor_tensor(
            out=theta[:],
            in0=inv_freq[:].unsqueeze(1).to_broadcast(table_shape),
            in1=position[:].unsqueeze(2).to_broadcast(table_shape),
            op=ALU.mult,
        )
        turns = consts.tile([P, TILES_PER_BATCH, 2, HEAD], F32)
        for plane, ahead in ((0, 0.25), (1, 0.0)):
            nc.vector.tensor_scalar(
                out=turns[:, :, plane, :],
                in0=theta[:],
                scalar1=1.0 / (2.0 * math.pi),
                scalar2=ahead,
                op0=ALU.mult,
                op1=ALU.add,
            )
        whole = consts.tile([P, TILES_PER_BATCH, 2, HEAD], F32)
        nc.vector.tensor_scalar(
            out=whole[:], in0=turns[:], scalar1=ROUND_MAGIC, scalar2=ROUND_MAGIC, op0=ALU.add, op1=ALU.subtract
        )
        fraction = consts.tile([P, TILES_PER_BATCH, 2, HEAD], F32)
        nc.vector.tensor_tensor(out=fraction[:], in0=turns[:], in1=whole[:], op=ALU.subtract)
        cos_sin = consts.tile([P, TILES_PER_BATCH, 2, HEAD], F32)

        def take_sines():
            nc.scalar.activation(out=cos_sin[:], in_=fraction[:], func=ACT.Sin, scale=2.0 * math.pi)
            nc.scalar.activation(out=warm[:, 1:2], in_=inv_freq[:, 0:1], func=ACT.Abs_reciprocal_sqrt)

        rope = consts.tile([P, TILES_PER_BATCH, STREAMS, 2, HEAD], F32)

        spread = {}

        def spread_gains():
            bank = psum_kv.tile([P, ROUND_TILES, STREAMS, KV], F32, name="product")
            nc.tensor.matmul(
                out=bank[:, 0, 0, :],
                lhsT=all_ones[:],
                rhs=gains_on_row_0[:].rearrange("p s j -> p (s j)"),
                start=True,
                stop=True,
            )
            spread["gains"] = bank[:, 0, 0, :].rearrange("p (s j) -> p s j", s=STREAMS)

        def finish_tables():
            gains = spread["gains"]
            nc.vector.tensor_tensor(
                out=rope[:, :, 0, :, :],
                in0=cos_sin[:],
                in1=gains[:, 0, :].unsqueeze(1).unsqueeze(1).to_broadcast([P, TILES_PER_BATCH, 2, HEAD]),
                op=ALU.mult,
            )
            gain_a = gains[:, 1, :].unsqueeze(1).to_broadcast(table_shape)
            nc.vector.scalar_tensor_tensor(
                out=rope[:, :, 1, 0, :], in0=cos_sin[:, :, 1, :], scalar=-1.0, in1=gain_a, op0=ALU.mult, op1=ALU.mult
            )
            nc.vector.tensor_tensor(out=rope[:, :, 1, 1, :], in0=cos_sin[:, :, 0, :], in1=gain_a, op=ALU.mult)

        last = ROUNDS - 1
        k_all = resident.tile([P, BATCH * TILES_PER_BATCH, KV], F32)
        v_all = resident.tile([P, BATCH * TILES_PER_BATCH, KV], F32)
        transposed = {}
        grouped = {}
        codes = {}
        planes = {}
        products = {}
        inv_norm = {}
        squares = {}
        unread = {}
        shares = {}

        sorted_words = {}

        def units(r):
            b, i = divmod(ROUND_TILES * r, TILES_PER_BATCH)
            together = any(first <= i and i + ROUND_TILES <= end for first, end in LOADS[b])
            if together and r != last:
                return [(t, s) for s in range(STREAMS) for t in range(ROUND_TILES)]
            return [(t, s) for t in range(ROUND_TILES) for s in range(STREAMS)]

        def sort_words(r, unit):
            t, s = units(r)[unit]
            b, i = divmod(ROUND_TILES * r + t, TILES_PER_BATCH)
            flat = stage.tile([P, PASSES, HALVES, P], F32, name="flat")
            nc.vector.tensor_copy(
                out=flat[:],
                in_=acts[s][b][:, i, :].bitcast(F32).rearrange("p (g m u) -> p g u m", g=PASSES, u=HALVES),
            )
            sorted_words[(r, t, s)] = flat

        def transpose_round(r):
            for unit, (t, s) in enumerate(units(r)):
                b, i = divmod(ROUND_TILES * r + t, TILES_PER_BATCH)
                words = acts[s][b][:, i, :].bitcast(F32)
                bank = psum_t.tile([P, PASSES, HALVES, P], F32, name="bank")
                for g in range(PASSES):
                    for u in range(HALVES):
                        first = g * K_PASS // 2 + u
                        if (r, t, s) in sorted_words:
                            source = sorted_words[(r, t, s)][:, g, u, :]
                        else:
                            source = words[:, first : (g + 1) * K_PASS // 2 : HALVES]
                        nc.tensor.transpose(out=bank[:, g, u, :], in_=source, identity=identity[:])
                transposed[(r, unit)] = bank
            grouped[r] = stage.tile([P, UNITS, D_MODEL], BF16, name="grouped", align_bytes=64)

        def empty_bank(copy, r, unit):
            copy(
                out=grouped[r][:, unit, :].bitcast(F32).rearrange("p (g n u) -> p g n u", g=PASSES, u=HALVES),
                in_=transposed[(r, unit)][:].rearrange("p g u n -> p g n u"),
            )

        def quantise(r, first, count):
            if r not in codes:
                codes[r] = stage.tile([P, UNITS, D_MODEL // 4], U32, name="codes", align_bytes=64)
                planes[r] = stage.tile([P, UNITS, D_MODEL // 4], U8, name="planes", align_bytes=64)
            some = slice(first, first + count)
            nc.vector.quantize_mx(
                out=codes[r][:, some, :].rearrange("p u w -> p (u w)").bitcast(FP8X4),
                scales=planes[r][:, some, :].rearrange("p u w -> p (u w)"),
                in_=grouped[r][:, some, :].rearrange("p u k -> p (u k)"),
            )

        def multiply(r):
            bank = psum_kv.tile([P, ROUND_TILES, STREAMS, KV], F32, name="product")
            products[(r, 0)] = bank[:, 0, :, :]
            products[(r, 1)] = bank[:, 1, :, :]
            if r == last:
                other = psum_t.tile([P, PASSES, HALVES, P], F32, name="bank")
                products[(r, 1)] = other[:, 1, :, :]
            for unit, (t, s) in enumerate(units(r)):
                for g in range(PASSES):
                    tokens = slice(g * P, (g + 1) * P)
                    nc.tensor.matmul_mx(
                        out=products[(r, t)][:, s, :],
                        lhsT=codes[r][:, unit, tokens].bitcast(FP8X4),
                        lhsT_scale=planes[r][:, unit, tokens],
                        rhs=w_codes[:, s, g, :].bitcast(FP8X4),
                        rhs_scale=w_planes[:, s, g, :],
                        start=(g == 0),
                        stop=(g == PASSES - 1),
                    )

        def sum_squares(r, t):
            if r not in squares:
                squares[r] = small.tile([P, 2, ROUND_TILES * STREAMS], F32, name="square_sums")
                unread[r] = stage.tile([P, ROUND_TILES, STREAMS, HEAD], F32, name="unread")
                inv_norm[r] = small.tile([P, ROUND_TILES * STREAMS], F32, name="inverse_norms")
            for s in range(STREAMS):
                column = STREAMS * t + s
                nc.scalar.activation(
                    out=unread[r][:, t, s, :],
                    in_=products[(r, t)][:, s, 0:HEAD],
                    func=ACT.Square,
                    accum_out=squares[r][:, 0, column : column + 1],
                )

        def apply_floor(r, first, count):
            columns = slice(STREAMS * first, STREAMS * (first + count))
            nc.scalar.activation(
                out=squares[r][:, 1, columns], in_=squares[r][:, 0, columns], func=ACT.Relu, bias=floor_minus[:]
            )

        def invert_norms(r, first, count):
            columns = slice(STREAMS * first, STREAMS * (first + count))
            nc.scalar.activation(
                out=inv_norm[r][:, columns], in_=squares[r][:, 1, columns], func=ACT.Abs_reciprocal_sqrt, bias=floor_plus[:]
            )

        def rotate(r, t):
            if r not in shares:
                shares[r] = stage.tile([P, ROUND_TILES, STREAMS, 2, HEAD], F32, name="share")
            i = (ROUND_TILES * r + t) % TILES_PER_BATCH
            for s in range(STREAMS):
                column = STREAMS * t + s
                nc.vector.scalar_tensor_tensor(
                    out=shares[r][:, t, s, :, :],
                    in0=products[(r, t)][:, s, 0:HEAD].unsqueeze(1).to_broadcast([P, 2, HEAD]),
                    scalar=inv_norm[r][:, column : column + 1],
                    in1=rope[:, i, s, :, :],
                    op0=ALU.mult,
                    op1=ALU.mult,
                )

        def add_shares(engine, r, first, count):
            some = slice(first, first + count)
            engine.tensor_tensor(
                out=k_all[:, ROUND_TILES * r + first : ROUND_TILES * r + first + count, :],
                in0=shares[r][:, some, 0, :, :].rearrange("p t h j -> p t (h j)"),
                in1=shares[r][:, some, 1, :, :].rearrange("p t h j -> p t (h j)"),
                op=ALU.add,
            )

        def copy_values_of_tile(r, t):
            nc.scalar.copy(
                out=v_all[:, ROUND_TILES * r + t, :].rearrange("p (s j) -> p s j", s=STREAMS),
                in_=products[(r, t)][:, :, HEAD:KV],
            )

        pieces = [(TILES_PER_BATCH * b, TILES_PER_BATCH * (b + 1)) for b in range(BATCH - 2)]
        first_to_go = ROUNDS - 4
        pieces.append((TILES_PER_BATCH * (BATCH - 2), ROUND_TILES * (first_to_go + 1)))
        pieces.append((ROUND_TILES * (first_to_go + 1), TILES_PER_BATCH * (BATCH - 1)))
        pieces.append((TILES_PER_BATCH * (BATCH - 1), ROUND_TILES * last))
        pieces.append((ROUND_TILES * last, BATCH * TILES_PER_BATCH))

        held_back = []

        def store(out, result, first, end):
            b, i = divmod(first, TILES_PER_BATCH)
            nc.sync.dma_start(
                out=out[b].rearrange("(p i) c -> p i c", i=TILES_PER_BATCH)[:, i : i + end - first, :],
                in_=result[:, first:end, :],
            )

        def store_finished(out, result, r):
            for first, end in pieces:
                if (end - 1) // ROUND_TILES == r:
                    if r < first_to_go:
                        held_back.append((out, result, first, end))
                    else:
                        store(out, result, first, end)
                        for earlier in held_back:
                            store(earlier[0], earlier[1], earlier[2], earlier[3])
                        held_back.clear()

        for step in range(ROUNDS + 1):
            transposing = step < ROUNDS
            multiplying = 0 <= step - 1
            norming = 0 <= step - 2
            closing = 0 <= step - 3
            if transposing:
                transpose_round(step)
            if step == 0:
                spread_gains()
            if multiplying:
                if step - 1 == last:
                    quantise(last, 2, 1)
                    quantise(last, 3, 1)
                else:
                    quantise(step - 1, 2, 2)
                multiply(step - 1)

            if norming:
                sum_squares(step - 2, 0)
                sum_squares(step - 2, 1)
                copy_values_of_tile(step - 2, 0)
                apply_floor(step - 2, 0, ROUND_TILES)
                copy_values_of_tile(step - 2, 1)
                store_finished(out_1, v_all, step - 2)
                invert_norms(step - 2, 0, ROUND_TILES)
            if step == ROUNDS:
                sum_squares(last, 0)
                sum_squares(last, 1)
                copy_values_of_tile(last, 0)
                apply_floor(last, 0, ROUND_TILES)
                copy_values_of_tile(last, 1)
                store_finished(out_1, v_all, last)
                invert_norms(last, 0, ROUND_TILES)
            if transposing:
                for unit in range(1, UNITS):
                    empty_bank(nc.scalar.copy, step, unit)
            if step == 0:
                take_sines()

            if closing:
                rotate(step - 3, 1)
                add_shares(nc.gpsimd, step - 3, 0, ROUND_TILES)
                store_finished(out_0, k_all, step - 3)
            if transposing:
                empty_bank(nc.vector.tensor_copy, step, 0)
            if step == 1:
                finish_tables()
            if norming:
                rotate(step - 2, 0)
            if transposing:
                quantise(step, 0, 2)
            if 2 <= step + 1 < ROUNDS - 3:
                sort_words(step + 1, UNITS - 1)
            if step == ROUNDS:
                rotate(step - 2, 1)
                add_shares(nc.gpsimd, step - 2, 0, ROUND_TILES)
                store_finished(out_0, k_all, step - 2)
                for t in range(ROUND_TILES):
                    rotate(last, t)
                for t in range(ROUND_TILES):
                    add_shares(nc.vector, last, t, 1)
                store_finished(out_0, k_all, last)
